import numpy as np
import ml_dtypes


def mxq(x, axis, fmt="e4m3"):
    dtype, down = {"e4m3": (ml_dtypes.float8_e4m3fn, 7), "e5m2": (ml_dtypes.float8_e5m2, 14)}[fmt]
    v = np.moveaxis(np.asarray(x, np.float32).astype(ml_dtypes.bfloat16).astype(np.float64), axis, -1)
    blocks = v.reshape(v.shape[:-1] + (-1, 32))
    amax = np.abs(blocks).max(-1, keepdims=True)
    byte = np.maximum(np.where(amax > 0, np.frexp(amax)[1] - 1 + 127, 0) - down, 1)
    scale = np.exp2(byte - 127.0)
    codes = (blocks / scale).astype(np.float32).astype(dtype).astype(np.float64)
    return np.moveaxis((codes * scale).reshape(v.shape), -1, axis)


WIDE = False


def mx_kscale(k):
    if not WIDE:
        return np.ones(k)
    levels = np.array([10, -10, 5, -5, 0])
    a = np.random.permutation(np.resize(levels, k // 512 * 4)).reshape(k // 512, 4)
    idx = np.arange(k)
    return np.exp2(a[idx // 512, idx % 128 // 32])


BF16 = ml_dtypes.bfloat16


def bf(x):
    return np.asarray(x, np.float32).astype(BF16)


def f64(x):
    return np.asarray(x).astype(np.float64)


E2M1 = np.array([0.0, 0.5, 1.0, 1.5, 2.0, 3.0, 4.0, 6.0, -0.0, -0.5, -1.0, -1.5, -2.0, -3.0, -4.0, -6.0])


def pack_weight(w, fmt):
    k, n = w.shape
    w = f64(bf(w)).reshape(k // 32, 32, n)
    amax = np.abs(w).max(1)
    if fmt == "e4m3":
        byte = np.frexp(amax)[1] - 1 + 127 - 7
    else:
        mant, ex = np.frexp(amax / 6.0)
        byte = np.where(mant > 0.5, ex, ex - 1) + 127
    byte = np.clip(np.where(amax > 0, byte, 1), 1, 254)
    scaled = (w * np.exp2(127.0 - byte)[:, None, :]).reshape(k, n).astype(np.float32)
    by_word = np.ascontiguousarray(scaled.reshape(k // 512, 128, 4, n).transpose(0, 1, 3, 2))
    if fmt == "e4m3":
        words = by_word.astype(ml_dtypes.float8_e4m3fn).view(np.uint8)
    else:
        c = by_word.astype(ml_dtypes.float4_e2m1fn).view(np.uint8) & 0xF
        words = c[..., 0::2] | (c[..., 1::2] << 4)
    return np.ascontiguousarray(words), np.ascontiguousarray(byte.astype(np.uint8).reshape(k // 512, 16, n))


def unpack_weight(words, scales, fmt):
    g, p, n, _ = words.shape
    if fmt == "e4m3":
        vals = np.ascontiguousarray(words).view(ml_dtypes.float8_e4m3fn).astype(np.float64)
    else:
        nib = np.empty((g, p, n, 4), np.uint8)
        nib[..., 0::2] = words & 0xF
        nib[..., 1::2] = words >> 4
        vals = E2M1[nib]
    vals = vals * np.repeat(np.exp2(scales.astype(np.float64) - 127.0), 8, axis=1)[..., None]
    return vals.transpose(0, 1, 3, 2).reshape(g * 512, n)

def pack4(w):
    words, scales = pack_weight(w, "e2m1")
    return words.reshape(words.shape[0], 128, -1), scales


def unpack4(words, scales):
    return unpack_weight(words.reshape(words.shape[0], 128, -1, 2), scales, "e2m1")


B, N, DIM, H, DH = 2, 64, 8192, 16, 96
D1 = DH // 3


def rotate_half(t):
    d = t.shape[-1]
    t1, t2 = t[..., : (d + 1) // 2], t[..., (d + 1) // 2:]
    return np.concatenate((-t2, t1), axis=-1)


def apply_rope(t, freqs):
    return t * np.cos(freqs) + rotate_half(t) * np.sin(freqs)


def rope3(t, fs):
    return np.concatenate([apply_rope(ts, f) for ts, f in zip(np.split(t, (D1, 2 * D1), axis=-1), fs)], axis=-1)


def setup_inputs():
    s = mx_kscale(DIM)
    x = bf(np.random.standard_normal((B, N, DIM)) * s)
    f1 = bf(np.random.uniform(0.0, 1.0, (N, D1)))
    f2 = bf(np.random.uniform(0.0, 1.0, (N, D1)))
    f3 = bf(np.random.uniform(0.0, 1.0, (N, D1)))
    words, scales = pack4(np.random.standard_normal((DIM, 3 * H * DH)) / np.sqrt(DIM) / s[:, None])
    return {"x": x, "f1": f1, "f2": f2, "f3": f3, "Wqkv_words": words, "Wqkv_scales": scales}


def reference(x, f1, f2, f3, Wqkv_words, Wqkv_scales):
    qkv = mxq(f64(x), 2, "e4m3") @ unpack4(Wqkv_words, Wqkv_scales)
    q, k, v = np.split(qkv, 3, axis=-1)
    to_heads = lambda t: t.reshape(B, N, H, DH).transpose(0, 2, 1, 3)
    q, k, v = to_heads(q), to_heads(k), to_heads(v)
    fs = (f64(f1), f64(f2), f64(f3))
    return rope3(q, fs), rope3(k, fs), v

@@ -1,0 +1,185 @@
+from contextlib import ExitStack
+
+import concourse.mybir as mybir
+from concourse.masks import make_identity
+
+F32 = mybir.dt.float32
+BF16 = mybir.dt.bfloat16
+I32 = mybir.dt.int32
+U32 = mybir.dt.uint32
+U8 = mybir.dt.uint8
+FP8X4 = mybir.dt.float8_e4m3fn_x4
+FP4X4 = mybir.dt.float4_e2m1fn_x4
+SIN = mybir.ActivationFunctionType.Sin
+
+P = 128
+K = 8192
+K_PASS = 512
+PASSES = K // K_PASS
+HEADS = 16
+HEAD = 96
+ROPE = 32
+TOKENS_PER_BATCH = 64
+PART = HEADS * HEAD
+BANK = 512
+BANKS = PART // BANK
+CHUNK = 4
+X_PIECE = 4
+TABLE = BANK + (BANKS - 1) * ROPE
+
+FLOPS = 2 * P * K * 3 * PART
+
+
+def tile_attention_pa_k_kernel(tc, x, f1, f2, f3, Wqkv_words, Wqkv_scales, out_0, out_1, out_2):
+    nc = tc.nc
+    outs = (out_0, out_1, out_2)
+    words_i32 = Wqkv_words.bitcast(I32)
+    scales_i32 = Wqkv_scales.bitcast(I32)
+    x_rows = x.flatten_outer_dims()
+
+    with ExitStack() as ctx:
+        ctx.enter_context(tc.manual_schedule())
+        keep = ctx.enter_context(tc.tile_pool(name="keep", bufs=1))
+        x_pool = ctx.enter_context(tc.tile_pool(name="x_pool", bufs=K // (K_PASS * X_PIECE)))
+        stage = ctx.enter_context(tc.tile_pool(name="stage", bufs=2))
+        w_pool = ctx.enter_context(tc.tile_pool(name="w_pool", bufs=2 * PASSES // CHUNK))
+        psum = ctx.enter_context(tc.psum_pool(name="psum", bufs=2))
+
+        x_pieces = []
+        for piece in range(PASSES // X_PIECE):
+            x_piece = x_pool.tile([P, X_PIECE * K_PASS], BF16)
+            cols = slice(piece * X_PIECE * K_PASS, (piece + 1) * X_PIECE * K_PASS)
+            nc.sync.dma_start(out=x_piece[:], in_=x_rows[:, cols])
+            x_pieces.append(x_piece)
+
+        planes = []
+        for i in range(2):
+            plane = keep.tile([P, PASSES, PART], U8, name="plane%d" % i, align_bytes=64)
+            nc.vector.memset(plane[:].bitcast(I32), 0)
+            planes.append(plane)
+
+        def load_round(r):
+            plane = planes[r % 2]
+            cols = slice(r * PART // 4, (r + 1) * PART // 4)
+            for g_half in range(2):
+                gs = slice(g_half * PASSES // 2, (g_half + 1) * PASSES // 2)
+                for low in range(8):
+                    first = 32 * (low // 4) + low % 4
+                    nc.sync.dma_start(
+                        out=plane[first:P:64, gs, :].bitcast(I32),
+                        in_=scales_i32[gs, low:16:8, cols].rearrange("g q c -> q g c"),
+                    )
+            chunks = []
+            cols = slice(r * PART // 2, (r + 1) * PART // 2)
+            for chunk in range(PASSES // CHUNK):
+                w_chunk = w_pool.tile([P, CHUNK, 2 * PART], U8, align_bytes=64)
+                gs = slice(chunk * CHUNK, (chunk + 1) * CHUNK)
+                nc.sync.dma_start(
+                    out=w_chunk[:].bitcast(I32),
+                    in_=words_i32[gs, :, cols].rearrange("g p c -> p g c"),
+                )
+                chunks.append(w_chunk)
+            return chunks
+
+        loaded = load_round(0)
+
+        angles = keep.tile([P, HEAD], BF16)
+        for b in range(2):
+            rows = slice(b * TOKENS_PER_BATCH, (b + 1) * TOKENS_PER_BATCH)
+            for a, f in enumerate((f1, f2, f3)):
+                nc.scalar.dma_start(out=angles[rows, a * ROPE : (a + 1) * ROPE], in_=f)
+        halves = "p (a h j) -> p a h j"
+        angles_v = angles[:].rearrange(halves, h=2, j=ROPE // 2)
+        sin_head = keep.tile([P, HEAD], F32)
+        sin_head_v = sin_head[:].rearrange(halves, h=2, j=ROPE // 2)
+        nc.scalar.activation(out=sin_head_v[:, :, 0, :], in_=angles_v[:, :, 0, :], func=SIN, scale=-1.0)
+        nc.scalar.activation(out=sin_head_v[:, :, 1, :], in_=angles_v[:, :, 1, :], func=SIN, scale=1.0)
+        cos_head = keep.tile([P, HEAD], F32)
+        nc.scalar.activation(out=cos_head[:], in_=angles[:], func=SIN, scale=0.5)
+        nc.vector.tensor_mul(out=cos_head[:], in0=cos_head[:], in1=cos_head[:])
+        nc.vector.tensor_scalar(
+            out=cos_head[:], in0=cos_head[:], scalar1=-2.0, scalar2=1.0,
+            op0=mybir.AluOpType.mult, op1=mybir.AluOpType.add,
+        )
+        cos_tab = keep.tile([P, TABLE], F32)
+        sin_tab = keep.tile([P, TABLE], F32)
+        for tab, head in ((cos_tab, cos_head), (sin_tab, sin_head)):
+            nc.vector.tensor_copy(
+                out=tab[:].rearrange("p (w c) -> p w c", c=HEAD),
+                in_=head[:].unsqueeze(1).to_broadcast([P, TABLE // HEAD, HEAD]),
+            )
+
+        ident = keep.tile([P, P], F32)
+        make_identity(nc, ident[:])
+        x_codes = keep.tile([P, PASSES, P], U32, align_bytes=64)
+        x_scales = keep.tile([P, PASSES, P], U8, align_bytes=64)
+        for piece, x_piece in enumerate(x_pieces):
+            x_words = x_piece[:].bitcast(F32)
+            grouped = stage.tile([P, X_PIECE, P, 2], F32, align_bytes=64)
+            for pair in range(X_PIECE // 2):
+                turned = psum.tile([P, 2, 2, P], F32)
+                for i in range(2):
+                    first_word = (2 * pair + i) * K_PASS // 2
+                    for u in range(2):
+                        nc.tensor.transpose(
+                            turned[:, i, u, :],
+                            x_words[:, first_word + u : first_word + K_PASS // 2 : 2],
+                            ident[:],
+                        )
+                nc.scalar.copy(
+                    out=grouped[:, 2 * pair : 2 * pair + 2, :, :],
+                    in_=turned[:].rearrange("p g u r -> p g r u"),
+                )
+            gs = slice(piece * X_PIECE, (piece + 1) * X_PIECE)
+            nc.vector.quantize_mx(
+                out=x_codes[:, gs, :].rearrange("p g r -> p (g r)").bitcast(FP8X4),
+                scales=x_scales[:, gs, :].rearrange("p g r -> p (g r)"),
+                in_=grouped[:].rearrange("p g r u -> p (g r u)").bitcast(BF16),
+            )
+
+        for r in range(3):
+            chunks = loaded
+            if r + 1 < 3:
+                loaded = load_round(r + 1)
+            plane = planes[r % 2]
+            accs = []
+            for c in range(BANKS):
+                acc = psum.tile([P, BANK], F32, name="acc%d" % c, tag="acc", bufs=2 * BANKS)
+                accs.append(acc)
+            for g in range(PASSES):
+                w_chunk = chunks[g // CHUNK]
+                for c in range(BANKS):
+                    nc.tensor.matmul_mx(
+                        out=accs[c][:],
+                        lhsT=x_codes[:, g, :].bitcast(FP8X4),
+                        lhsT_scale=x_scales[:, g, :],
+                        rhs=w_chunk[:, g % CHUNK, 2 * BANK * c : 2 * BANK * (c + 1)].bitcast(FP4X4),
+                        rhs_scale=plane[:, g, BANK * c : BANK * (c + 1)],
+                        start=(g == 0),
+                        stop=(g == PASSES - 1),
+                    )
+
+            result = stage.tile([P, PART], F32)
+            for c in range(BANKS):
+                cols = slice(c * BANK, (c + 1) * BANK)
+                if r == 2 and c % 2 == 0:
+                    nc.scalar.copy(out=result[:, cols], in_=accs[c][:])
+                elif r == 2:
+                    nc.vector.tensor_copy(out=result[:, cols], in_=accs[c][:])
+                else:
+                    window = slice(c * ROPE, c * ROPE + BANK)
+                    acc_v = accs[c][:].rearrange(halves, h=2, j=ROPE // 2)
+                    sin_v = sin_tab[:, window].rearrange(halves, h=2, j=ROPE // 2)
+                    own = stage.tile([P, BANK], F32)
+                    partner = stage.tile([P, BANK], F32)
+                    partner_v = partner[:].rearrange(halves, h=2, j=ROPE // 2)
+                    nc.vector.tensor_mul(out=own[:], in0=accs[c][:], in1=cos_tab[:, window])
+                    nc.vector.tensor_mul(out=partner_v[:, :, 0, :], in0=acc_v[:, :, 1, :], in1=sin_v[:, :, 0, :])
+                    nc.vector.tensor_mul(out=partner_v[:, :, 1, :], in0=acc_v[:, :, 0, :], in1=sin_v[:, :, 1, :])
+                    nc.vector.tensor_add(out=result[:, cols], in0=own[:], in1=partner[:])
+            for b in range(2):
+                rows = slice(b * TOKENS_PER_BATCH, (b + 1) * TOKENS_PER_BATCH)
+                nc.scalar.dma_start(
+                    out=outs[r][b].rearrange("h n d -> n h d"),
+                    in_=result[rows, :].rearrange("n (h d) -> n h d", d=HEAD),
+                )

@@ -61,13 +61,12 @@ def tile_attention_pa_k_kernel(tc, x, f1, f2, f3, Wqkv_words, Wqkv_scales, out_0
         def load_round(r):
             plane = planes[r % 2]
             cols = slice(r * PART // 4, (r + 1) * PART // 4)
-            for g_half in range(2):
-                gs = slice(g_half * PASSES // 2, (g_half + 1) * PASSES // 2)
-                for low in range(8):
-                    first = 32 * (low // 4) + low % 4
+            for low in range(8):
+                for q in (low, low + 8):
+                    row = 32 * (q // 4) + q % 4
                     nc.sync.dma_start(
-                        out=plane[first:P:64, gs, :].bitcast(I32),
-                        in_=scales_i32[gs, low:16:8, cols].rearrange("g q c -> q g c"),
+                        out=plane[row : row + 1, :, :].bitcast(I32),
+                        in_=scales_i32[:, q : q + 1, cols].rearrange("g o c -> o g c"),
                     )
             chunks = []
             cols = slice(r * PART // 2, (r + 1) * PART // 2)

@@ -24,7 +24,7 @@ PART = HEADS * HEAD
 BANK = 512
 BANKS = PART // BANK
 CHUNK = 4
-X_PIECE = 4
+X_PIECE = 8
 TABLE = BANK + (BANKS - 1) * ROPE
 
 FLOPS = 2 * P * K * 3 * PART
@@ -45,6 +45,12 @@ def tile_attention_pa_k_kernel(tc, x, f1, f2, f3, Wqkv_words, Wqkv_scales, out_0
         w_pool = ctx.enter_context(tc.tile_pool(name="w_pool", bufs=2 * PASSES // CHUNK))
         psum = ctx.enter_context(tc.psum_pool(name="psum", bufs=2))
 
+        angles = keep.tile([P, HEAD], BF16)
+        for b in range(2):
+            rows = slice(b * TOKENS_PER_BATCH, (b + 1) * TOKENS_PER_BATCH)
+            for a, f in enumerate((f1, f2, f3)):
+                nc.scalar.dma_start(out=angles[rows, a * ROPE : (a + 1) * ROPE], in_=f)
+
         x_pieces = []
         for piece in range(PASSES // X_PIECE):
             x_piece = x_pool.tile([P, X_PIECE * K_PASS], BF16)
@@ -61,13 +67,11 @@ def tile_attention_pa_k_kernel(tc, x, f1, f2, f3, Wqkv_words, Wqkv_scales, out_0
         def load_round(r):
             plane = planes[r % 2]
             cols = slice(r * PART // 4, (r + 1) * PART // 4)
-            for low in range(8):
-                for q in (low, low + 8):
-                    row = 32 * (q // 4) + q % 4
-                    nc.sync.dma_start(
-                        out=plane[row : row + 1, :, :].bitcast(I32),
-                        in_=scales_i32[:, q : q + 1, cols].rearrange("g o c -> o g c"),
-                    )
+            for i in range(4):
+                nc.sync.dma_start(
+                    out=plane[i:P:32, :, :].bitcast(I32),
+                    in_=scales_i32[:, i:16:4, cols].rearrange("g q c -> q g c"),
+                )
             chunks = []
             cols = slice(r * PART // 2, (r + 1) * PART // 2)
             for chunk in range(PASSES // CHUNK):
@@ -82,11 +86,6 @@ def tile_attention_pa_k_kernel(tc, x, f1, f2, f3, Wqkv_words, Wqkv_scales, out_0
 
         loaded = load_round(0)
 
-        angles = keep.tile([P, HEAD], BF16)
-        for b in range(2):
-            rows = slice(b * TOKENS_PER_BATCH, (b + 1) * TOKENS_PER_BATCH)
-            for a, f in enumerate((f1, f2, f3)):
-                nc.scalar.dma_start(out=angles[rows, a * ROPE : (a + 1) * ROPE], in_=f)
         halves = "p (a h j) -> p a h j"
         angles_v = angles[:].rearrange(halves, h=2, j=ROPE // 2)
         sin_head = keep.tile([P, HEAD], F32)

@@ -67,10 +67,11 @@ def tile_attention_pa_k_kernel(tc, x, f1, f2, f3, Wqkv_words, Wqkv_scales, out_0
         def load_round(r):
             plane = planes[r % 2]
             cols = slice(r * PART // 4, (r + 1) * PART // 4)
-            for i in range(4):
+            for q in range(8):
+                row = 32 * (q // 4) + q % 4
                 nc.sync.dma_start(
-                    out=plane[i:P:32, :, :].bitcast(I32),
-                    in_=scales_i32[:, i:16:4, cols].rearrange("g q c -> q g c"),
+                    out=plane[row:P:64, :, :].bitcast(I32),
+                    in_=scales_i32[:, q:16:8, cols].rearrange("g q c -> q g c"),
                 )
             chunks = []
             cols = slice(r * PART // 2, (r + 1) * PART // 2)

@@ -67,16 +67,20 @@ def tile_attention_pa_k_kernel(tc, x, f1, f2, f3, Wqkv_words, Wqkv_scales, out_0
         def load_round(r):
             plane = planes[r % 2]
             cols = slice(r * PART // 4, (r + 1) * PART // 4)
-            for q in range(8):
-                row = 32 * (q // 4) + q % 4
-                nc.sync.dma_start(
-                    out=plane[row:P:64, :, :].bitcast(I32),
-                    in_=scales_i32[:, q:16:8, cols].rearrange("g q c -> q g c"),
-                )
+            for gs in (slice(0, CHUNK), slice(CHUNK, PASSES)):
+                for i in range(4):
+                    nc.sync.dma_start(
+                        out=plane[i:P:32, gs, :].bitcast(I32),
+                        in_=scales_i32[gs, i:16:4, cols].rearrange("g q c -> q g c"),
+                    )
             chunks = []
             cols = slice(r * PART // 2, (r + 1) * PART // 2)
             for chunk in range(PASSES // CHUNK):
                 w_chunk = w_pool.tile([P, CHUNK, 2 * PART], U8, align_bytes=64)
+                if chunk == 0:
+                    nc.vector.tensor_copy(
+                        out=w_chunk[0:4, 0, 0:4].bitcast(I32), in_=plane[0:4, 0, 0:4].bitcast(I32)
+                    )
                 gs = slice(chunk * CHUNK, (chunk + 1) * CHUNK)
                 nc.sync.dma_start(
                     out=w_chunk[:].bitcast(I32),

@@ -20,14 +20,18 @@ HEADS = 16
 HEAD = 96
 ROPE = 32
 TOKENS_PER_BATCH = 64
+ROUNDS = 3
 PART = HEADS * HEAD
 BANK = 512
 BANKS = PART // BANK
-CHUNK = 4
 X_PIECE = 8
+SCALE_PIECE = 4
+CHUNK = 2
+CHUNKS = PASSES // CHUNK
+AHEAD = 11
 TABLE = BANK + (BANKS - 1) * ROPE
 
-FLOPS = 2 * P * K * 3 * PART
+FLOPS = 2 * P * K * ROUNDS * PART
 
 
 def tile_attention_pa_k_kernel(tc, x, f1, f2, f3, Wqkv_words, Wqkv_scales, out_0, out_1, out_2):
@@ -40,9 +44,9 @@ def tile_attention_pa_k_kernel(tc, x, f1, f2, f3, Wqkv_words, Wqkv_scales, out_0
     with ExitStack() as ctx:
         ctx.enter_context(tc.manual_schedule())
         keep = ctx.enter_context(tc.tile_pool(name="keep", bufs=1))
-        x_pool = ctx.enter_context(tc.tile_pool(name="x_pool", bufs=K // (K_PASS * X_PIECE)))
+        x_pool = ctx.enter_context(tc.tile_pool(name="x_pool", bufs=PASSES // X_PIECE))
         stage = ctx.enter_context(tc.tile_pool(name="stage", bufs=2))
-        w_pool = ctx.enter_context(tc.tile_pool(name="w_pool", bufs=2 * PASSES // CHUNK))
+        w_pool = ctx.enter_context(tc.tile_pool(name="w_pool", bufs=AHEAD + 1))
         psum = ctx.enter_context(tc.psum_pool(name="psum", bufs=2))
 
         angles = keep.tile([P, HEAD], BF16)
@@ -58,38 +62,34 @@ def tile_attention_pa_k_kernel(tc, x, f1, f2, f3, Wqkv_words, Wqkv_scales, out_0
             nc.sync.dma_start(out=x_piece[:], in_=x_rows[:, cols])
             x_pieces.append(x_piece)
 
-        planes = []
-        for i in range(2):
-            plane = keep.tile([P, PASSES, PART], U8, name="plane%d" % i, align_bytes=64)
-            nc.vector.memset(plane[:].bitcast(I32), 0)
-            planes.append(plane)
-
-        def load_round(r):
-            plane = planes[r % 2]
-            cols = slice(r * PART // 4, (r + 1) * PART // 4)
-            for gs in (slice(0, CHUNK), slice(CHUNK, PASSES)):
-                for i in range(4):
-                    nc.sync.dma_start(
-                        out=plane[i:P:32, gs, :].bitcast(I32),
-                        in_=scales_i32[gs, i:16:4, cols].rearrange("g q c -> q g c"),
-                    )
-            chunks = []
-            cols = slice(r * PART // 2, (r + 1) * PART // 2)
-            for chunk in range(PASSES // CHUNK):
-                w_chunk = w_pool.tile([P, CHUNK, 2 * PART], U8, align_bytes=64)
-                if chunk == 0:
-                    nc.vector.tensor_copy(
-                        out=w_chunk[0:4, 0, 0:4].bitcast(I32), in_=plane[0:4, 0, 0:4].bitcast(I32)
-                    )
-                gs = slice(chunk * CHUNK, (chunk + 1) * CHUNK)
+        plane = keep.tile([P, PASSES, ROUNDS * PART], U8, align_bytes=64)
+        for piece in range(PASSES // SCALE_PIECE):
+            gs = slice(piece * SCALE_PIECE, (piece + 1) * SCALE_PIECE)
+            nc.vector.memset(plane[:, gs, :].bitcast(I32), 0)
+            for i in range(4):
                 nc.sync.dma_start(
-                    out=w_chunk[:].bitcast(I32),
-                    in_=words_i32[gs, :, cols].rearrange("g p c -> p g c"),
+                    out=plane[i:P:32, gs, :].bitcast(I32),
+                    in_=scales_i32[gs, i:16:4, :].rearrange("g q c -> q g c"),
                 )
-                chunks.append(w_chunk)
-            return chunks
 
-        loaded = load_round(0)
+        def load_weights(j):
+            r = j // CHUNKS
+            gs = slice(j % CHUNKS * CHUNK, (j % CHUNKS + 1) * CHUNK)
+            w_chunk = w_pool.tile([P, CHUNK, 2 * PART], U8, align_bytes=64)
+            if j == 0:
+                held_by = PASSES - 2 * SCALE_PIECE
+                nc.vector.tensor_copy(
+                    out=w_chunk[0:4, 0, 0:4].bitcast(I32), in_=plane[0:4, held_by, 0:4].bitcast(I32)
+                )
+            nc.sync.dma_start(
+                out=w_chunk[:].bitcast(I32),
+                in_=words_i32[gs, :, r * PART // 2 : (r + 1) * PART // 2].rearrange("g p c -> p g c"),
+            )
+            return w_chunk
+
+        w_chunks = []
+        for j in range(AHEAD):
+            w_chunks.append(load_weights(j))
 
         halves = "p (a h j) -> p a h j"
         angles_v = angles[:].rearrange(halves, h=2, j=ROPE // 2)
@@ -140,24 +140,23 @@ def tile_attention_pa_k_kernel(tc, x, f1, f2, f3, Wqkv_words, Wqkv_scales, out_0
                 in_=grouped[:].rearrange("p g r u -> p (g r u)").bitcast(BF16),
             )
 
-        for r in range(3):
-            chunks = loaded
-            if r + 1 < 3:
-                loaded = load_round(r + 1)
-            plane = planes[r % 2]
+        for r in range(ROUNDS):
             accs = []
             for c in range(BANKS):
                 acc = psum.tile([P, BANK], F32, name="acc%d" % c, tag="acc", bufs=2 * BANKS)
                 accs.append(acc)
             for g in range(PASSES):
-                w_chunk = chunks[g // CHUNK]
+                j = r * CHUNKS + g // CHUNK
+                if g % CHUNK == 0 and j + AHEAD < ROUNDS * CHUNKS:
+                    w_chunks.append(load_weights(j + AHEAD))
                 for c in range(BANKS):
+                    first_col = r * PART + c * BANK
                     nc.tensor.matmul_mx(
                         out=accs[c][:],
                         lhsT=x_codes[:, g, :].bitcast(FP8X4),
                         lhsT_scale=x_scales[:, g, :],
-                        rhs=w_chunk[:, g % CHUNK, 2 * BANK * c : 2 * BANK * (c + 1)].bitcast(FP4X4),
-                        rhs_scale=plane[:, g, BANK * c : BANK * (c + 1)],
+                        rhs=w_chunks[j][:, g % CHUNK, 2 * BANK * c : 2 * BANK * (c + 1)].bitcast(FP4X4),
+                        rhs_scale=plane[:, g, first_col : first_col + BANK],
                         start=(g == 0),
                         stop=(g == PASSES - 1),
                     )

@@ -19,7 +19,6 @@ PASSES = K // K_PASS
 HEADS = 16
 HEAD = 96
 ROPE = 32
-TOKENS_PER_BATCH = 64
 ROUNDS = 3
 PART = HEADS * HEAD
 BANK = 512
@@ -39,7 +38,6 @@ def tile_attention_pa_k_kernel(tc, x, f1, f2, f3, Wqkv_words, Wqkv_scales, out_0
     outs = (out_0, out_1, out_2)
     words_i32 = Wqkv_words.bitcast(I32)
     scales_i32 = Wqkv_scales.bitcast(I32)
-    x_rows = x.flatten_outer_dims()
 
     with ExitStack() as ctx:
         ctx.enter_context(tc.manual_schedule())
@@ -49,17 +47,19 @@ def tile_attention_pa_k_kernel(tc, x, f1, f2, f3, Wqkv_words, Wqkv_scales, out_0
         w_pool = ctx.enter_context(tc.tile_pool(name="w_pool", bufs=AHEAD + 1))
         psum = ctx.enter_context(tc.psum_pool(name="psum", bufs=2))
 
+        batch_rows = [slice(b, P, 2) for b in range(2)]
+
         angles = keep.tile([P, HEAD], BF16)
         for b in range(2):
-            rows = slice(b * TOKENS_PER_BATCH, (b + 1) * TOKENS_PER_BATCH)
             for a, f in enumerate((f1, f2, f3)):
-                nc.scalar.dma_start(out=angles[rows, a * ROPE : (a + 1) * ROPE], in_=f)
+                nc.scalar.dma_start(out=angles[batch_rows[b], a * ROPE : (a + 1) * ROPE], in_=f)
 
         x_pieces = []
         for piece in range(PASSES // X_PIECE):
             x_piece = x_pool.tile([P, X_PIECE * K_PASS], BF16)
             cols = slice(piece * X_PIECE * K_PASS, (piece + 1) * X_PIECE * K_PASS)
-            nc.sync.dma_start(out=x_piece[:], in_=x_rows[:, cols])
+            for b in range(2):
+                nc.sync.dma_start(out=x_piece[batch_rows[b], :], in_=x[b, :, cols])
             x_pieces.append(x_piece)
 
         plane = keep.tile([P, PASSES, ROUNDS * PART], U8, align_bytes=64)
@@ -180,8 +180,7 @@ def tile_attention_pa_k_kernel(tc, x, f1, f2, f3, Wqkv_words, Wqkv_scales, out_0
                     nc.vector.tensor_mul(out=partner_v[:, :, 1, :], in0=acc_v[:, :, 0, :], in1=sin_v[:, :, 1, :])
                     nc.vector.tensor_add(out=result[:, cols], in0=own[:], in1=partner[:])
             for b in range(2):
-                rows = slice(b * TOKENS_PER_BATCH, (b + 1) * TOKENS_PER_BATCH)
                 nc.scalar.dma_start(
                     out=outs[r][b].rearrange("h n d -> n h d"),
-                    in_=result[rows, :].rearrange("n (h d) -> n h d", d=HEAD),
+                    in_=result[batch_rows[b], :].rearrange("n (h d) -> n h d", d=HEAD),
                 )

@@ -24,7 +24,7 @@ PART = HEADS * HEAD
 BANK = 512
 BANKS = PART // BANK
 X_PIECE = 8
-SCALE_PIECE = 4
+SCALE_PIECE = 8
 CHUNK = 2
 CHUNKS = PASSES // CHUNK
 AHEAD = 11
@@ -66,10 +66,11 @@ def tile_attention_pa_k_kernel(tc, x, f1, f2, f3, Wqkv_words, Wqkv_scales, out_0
         for piece in range(PASSES // SCALE_PIECE):
             gs = slice(piece * SCALE_PIECE, (piece + 1) * SCALE_PIECE)
             nc.vector.memset(plane[:, gs, :].bitcast(I32), 0)
-            for i in range(4):
+            for q in range(8):
+                row = 32 * (q // 4) + q % 4
                 nc.sync.dma_start(
-                    out=plane[i:P:32, gs, :].bitcast(I32),
-                    in_=scales_i32[gs, i:16:4, :].rearrange("g q c -> q g c"),
+                    out=plane[row:P:64, gs, :].bitcast(I32),
+                    in_=scales_i32[gs, q:16:8, :].rearrange("g q c -> q g c"),
                 )
 
         def load_weights(j):
@@ -77,7 +78,7 @@ def tile_attention_pa_k_kernel(tc, x, f1, f2, f3, Wqkv_words, Wqkv_scales, out_0
             gs = slice(j % CHUNKS * CHUNK, (j % CHUNKS + 1) * CHUNK)
             w_chunk = w_pool.tile([P, CHUNK, 2 * PART], U8, align_bytes=64)
             if j == 0:
-                held_by = PASSES - 2 * SCALE_PIECE
+                held_by = PASSES - SCALE_PIECE
                 nc.vector.tensor_copy(
                     out=w_chunk[0:4, 0, 0:4].bitcast(I32), in_=plane[0:4, held_by, 0:4].bitcast(I32)
                 )

@@ -54,12 +54,12 @@ def tile_attention_pa_k_kernel(tc, x, f1, f2, f3, Wqkv_words, Wqkv_scales, out_0
             for a, f in enumerate((f1, f2, f3)):
                 nc.scalar.dma_start(out=angles[batch_rows[b], a * ROPE : (a + 1) * ROPE], in_=f)
 
+        x_rows = x.rearrange("b n k -> (b n) k")
         x_pieces = []
         for piece in range(PASSES // X_PIECE):
             x_piece = x_pool.tile([P, X_PIECE * K_PASS], BF16)
             cols = slice(piece * X_PIECE * K_PASS, (piece + 1) * X_PIECE * K_PASS)
-            for b in range(2):
-                nc.sync.dma_start(out=x_piece[batch_rows[b], :], in_=x[b, :, cols])
+            nc.sync.dma_start(out=x_piece[:], in_=x_rows[:, cols])
             x_pieces.append(x_piece)
 
         plane = keep.tile([P, PASSES, ROUNDS * PART], U8, align_bytes=64)
@@ -130,10 +130,11 @@ def tile_attention_pa_k_kernel(tc, x, f1, f2, f3, Wqkv_words, Wqkv_scales, out_0
                             x_words[:, first_word + u : first_word + K_PASS // 2 : 2],
                             ident[:],
                         )
-                nc.scalar.copy(
-                    out=grouped[:, 2 * pair : 2 * pair + 2, :, :],
-                    in_=turned[:].rearrange("p g u r -> p g r u"),
-                )
+                for i in range(2):
+                    nc.scalar.copy(
+                        out=grouped[:, 2 * pair + i, :, :].rearrange("p (n b) u -> p n b u", b=2),
+                        in_=turned[:, i, :, :].rearrange("p u (b n) -> p n b u", b=2),
+                    )
             gs = slice(piece * X_PIECE, (piece + 1) * X_PIECE)
             nc.vector.quantize_mx(
                 out=x_codes[:, gs, :].rearrange("p g r -> p (g r)").bitcast(FP8X4),

@@ -19,18 +19,20 @@ PASSES = K // K_PASS
 HEADS = 16
 HEAD = 96
 ROPE = 32
-ROUNDS = 3
+PARTS = 3
 PART = HEADS * HEAD
 BANK = 512
-BANKS = PART // BANK
+PART_BANKS = PART // BANK
+PSUM_BANKS = 8
 X_PIECE = 8
 SCALE_PIECE = 8
-CHUNK = 2
-CHUNKS = PASSES // CHUNK
-AHEAD = 11
-TABLE = BANK + (BANKS - 1) * ROPE
+ROUNDS = ((6, 1), (2, 4), (1, 4))
+AHEAD = 8
+LOAD_BYTES = 8192
+EARLY_HEADS = 2 * BANK // HEAD
+TABLE = BANK + (PART_BANKS - 1) * ROPE
 
-FLOPS = 2 * P * K * ROUNDS * PART
+FLOPS = 2 * P * K * PARTS * PART
 
 
 def tile_attention_pa_k_kernel(tc, x, f1, f2, f3, Wqkv_words, Wqkv_scales, out_0, out_1, out_2):
@@ -45,7 +47,7 @@ def tile_attention_pa_k_kernel(tc, x, f1, f2, f3, Wqkv_words, Wqkv_scales, out_0
         x_pool = ctx.enter_context(tc.tile_pool(name="x_pool", bufs=PASSES // X_PIECE))
         stage = ctx.enter_context(tc.tile_pool(name="stage", bufs=2))
         w_pool = ctx.enter_context(tc.tile_pool(name="w_pool", bufs=AHEAD + 1))
-        psum = ctx.enter_context(tc.psum_pool(name="psum", bufs=2))
+        psum = ctx.enter_context(tc.psum_pool(name="psum", bufs=PSUM_BANKS))
 
         batch_rows = [slice(b, P, 2) for b in range(2)]
 
@@ -62,7 +64,7 @@ def tile_attention_pa_k_kernel(tc, x, f1, f2, f3, Wqkv_words, Wqkv_scales, out_0
             nc.sync.dma_start(out=x_piece[:], in_=x_rows[:, cols])
             x_pieces.append(x_piece)
 
-        plane = keep.tile([P, PASSES, ROUNDS * PART], U8, align_bytes=64)
+        plane = keep.tile([P, PASSES, PARTS * PART], U8, align_bytes=64)
         for piece in range(PASSES // SCALE_PIECE):
             gs = slice(piece * SCALE_PIECE, (piece + 1) * SCALE_PIECE)
             nc.vector.memset(plane[:, gs, :].bitcast(I32), 0)
@@ -73,18 +75,27 @@ def tile_attention_pa_k_kernel(tc, x, f1, f2, f3, Wqkv_words, Wqkv_scales, out_0
                     in_=scales_i32[gs, q:16:8, :].rearrange("g q c -> q g c"),
                 )
 
+        loads = []
+        first_bank = 0
+        for banks, groups in ROUNDS:
+            for g in range(0, PASSES, groups):
+                loads.append((first_bank, banks, g, groups))
+            first_bank += banks
+
         def load_weights(j):
-            r = j // CHUNKS
-            gs = slice(j % CHUNKS * CHUNK, (j % CHUNKS + 1) * CHUNK)
-            w_chunk = w_pool.tile([P, CHUNK, 2 * PART], U8, align_bytes=64)
+            first, banks, g, groups = loads[j]
+            row = 2 * BANK * banks
+            w_chunk = w_pool.tile([P, LOAD_BYTES], U8, align_bytes=64)
             if j == 0:
                 held_by = PASSES - SCALE_PIECE
                 nc.vector.tensor_copy(
-                    out=w_chunk[0:4, 0, 0:4].bitcast(I32), in_=plane[0:4, held_by, 0:4].bitcast(I32)
+                    out=w_chunk[0:4, 0:4].bitcast(I32), in_=plane[0:4, held_by, 0:4].bitcast(I32)
                 )
             nc.sync.dma_start(
-                out=w_chunk[:].bitcast(I32),
-                in_=words_i32[gs, :, r * PART // 2 : (r + 1) * PART // 2].rearrange("g p c -> p g c"),
+                out=w_chunk[:, : groups * row].bitcast(I32).rearrange("p (g c) -> p g c", g=groups),
+                in_=words_i32[
+                    g : g + groups, :, first * BANK // 2 : (first + banks) * BANK // 2
+                ].rearrange("g p c -> p g c"),
             )
             return w_chunk
 
@@ -121,7 +132,7 @@ def tile_attention_pa_k_kernel(tc, x, f1, f2, f3, Wqkv_words, Wqkv_scales, out_0
             x_words = x_piece[:].bitcast(F32)
             grouped = stage.tile([P, X_PIECE, P, 2], F32, align_bytes=64)
             for pair in range(X_PIECE // 2):
-                turned = psum.tile([P, 2, 2, P], F32)
+                turned = psum.tile([P, 2, 2, P], F32, tag="bank")
                 for i in range(2):
                     first_word = (2 * pair + i) * K_PASS // 2
                     for u in range(2):
@@ -142,47 +153,75 @@ def tile_attention_pa_k_kernel(tc, x, f1, f2, f3, Wqkv_words, Wqkv_scales, out_0
                 in_=grouped[:].rearrange("p g r u -> p (g r u)").bitcast(BF16),
             )
 
-        for r in range(ROUNDS):
+        results = []
+        for part in range(PARTS):
+            result = keep.tile([P, PART], F32, name="result%d" % part)
+            results.append(result)
+
+        def store(part, b, heads, queue):
+            queue.dma_start(
+                out=outs[part][b, heads].rearrange("h n d -> n h d"),
+                in_=results[part][batch_rows[b], heads.start * HEAD : heads.stop * HEAD].rearrange(
+                    "n (h d) -> n h d", d=HEAD
+                ),
+            )
+
+        def rotate(bank, acc):
+            part, c = divmod(bank, PART_BANKS)
+            cols = slice(c * BANK, (c + 1) * BANK)
+            window = slice(c * ROPE, c * ROPE + BANK)
+            acc_v = acc[:].rearrange(halves, h=2, j=ROPE // 2)
+            sin_v = sin_tab[:, window].rearrange(halves, h=2, j=ROPE // 2)
+            own = stage.tile([P, BANK], F32)
+            partner = stage.tile([P, BANK], F32)
+            partner_v = partner[:].rearrange(halves, h=2, j=ROPE // 2)
+            nc.vector.tensor_mul(out=own[:], in0=acc[:], in1=cos_tab[:, window])
+            nc.vector.tensor_mul(out=partner_v[:, :, 0, :], in0=acc_v[:, :, 1, :], in1=sin_v[:, :, 0, :])
+            nc.vector.tensor_mul(out=partner_v[:, :, 1, :], in0=acc_v[:, :, 0, :], in1=sin_v[:, :, 1, :])
+            nc.vector.tensor_add(out=results[part][:, cols], in0=own[:], in1=partner[:])
+
+        j = -1
+        first_bank = 0
+        for banks, groups in ROUNDS:
             accs = []
-            for c in range(BANKS):
-                acc = psum.tile([P, BANK], F32, name="acc%d" % c, tag="acc", bufs=2 * BANKS)
+            for c in range(banks):
+                acc = psum.tile([P, BANK], F32, tag="bank")
                 accs.append(acc)
             for g in range(PASSES):
-                j = r * CHUNKS + g // CHUNK
-                if g % CHUNK == 0 and j + AHEAD < ROUNDS * CHUNKS:
-                    w_chunks.append(load_weights(j + AHEAD))
-                for c in range(BANKS):
-                    first_col = r * PART + c * BANK
+                if g % groups == 0:
+                    j += 1
+                    if j + AHEAD < len(loads):
+                        w_chunks.append(load_weights(j + AHEAD))
+                for c in range(banks):
+                    first_col = (first_bank + c) * BANK
+                    first_byte = 2 * BANK * (g % groups * banks + c)
                     nc.tensor.matmul_mx(
                         out=accs[c][:],
                         lhsT=x_codes[:, g, :].bitcast(FP8X4),
                         lhsT_scale=x_scales[:, g, :],
-                        rhs=w_chunks[j][:, g % CHUNK, 2 * BANK * c : 2 * BANK * (c + 1)].bitcast(FP4X4),
+                        rhs=w_chunks[j][:, first_byte : first_byte + 2 * BANK].bitcast(FP4X4),
                         rhs_scale=plane[:, g, first_col : first_col + BANK],
                         start=(g == 0),
                         stop=(g == PASSES - 1),
                     )
 
-            result = stage.tile([P, PART], F32)
-            for c in range(BANKS):
-                cols = slice(c * BANK, (c + 1) * BANK)
-                if r == 2 and c % 2 == 0:
-                    nc.scalar.copy(out=result[:, cols], in_=accs[c][:])
-                elif r == 2:
-                    nc.vector.tensor_copy(out=result[:, cols], in_=accs[c][:])
+            for c in range(banks):
+                bank = first_bank + c
+                part, place = divmod(bank, PART_BANKS)
+                cols = slice(place * BANK, (place + 1) * BANK)
+                if part < 2:
+                    rotate(bank, accs[c])
+                elif place == 0:
+                    nc.scalar.copy(out=results[part][:, cols], in_=accs[c][:])
                 else:
-                    window = slice(c * ROPE, c * ROPE + BANK)
-                    acc_v = accs[c][:].rearrange(halves, h=2, j=ROPE // 2)
-                    sin_v = sin_tab[:, window].rearrange(halves, h=2, j=ROPE // 2)
-                    own = stage.tile([P, BANK], F32)
-                    partner = stage.tile([P, BANK], F32)
-                    partner_v = partner[:].rearrange(halves, h=2, j=ROPE // 2)
-                    nc.vector.tensor_mul(out=own[:], in0=accs[c][:], in1=cos_tab[:, window])
-                    nc.vector.tensor_mul(out=partner_v[:, :, 0, :], in0=acc_v[:, :, 1, :], in1=sin_v[:, :, 0, :])
-                    nc.vector.tensor_mul(out=partner_v[:, :, 1, :], in0=acc_v[:, :, 0, :], in1=sin_v[:, :, 1, :])
-                    nc.vector.tensor_add(out=result[:, cols], in0=own[:], in1=partner[:])
-            for b in range(2):
-                nc.scalar.dma_start(
-                    out=outs[r][b].rearrange("h n d -> n h d"),
-                    in_=result[batch_rows[b], :].rearrange("n (h d) -> n h d", d=HEAD),
-                )
+                    nc.vector.tensor_copy(out=results[part][:, cols], in_=accs[c][:])
+                if part < 2 and place == PART_BANKS - 1:
+                    for b in range(2):
+                        store(part, b, slice(0, HEADS), (nc.scalar, nc.sync)[part])
+                elif bank == PARTS * PART_BANKS - 2:
+                    for b in range(2):
+                        store(part, b, slice(0, EARLY_HEADS), (nc.scalar, nc.sync)[b])
+                elif bank == PARTS * PART_BANKS - 1:
+                    for b in range(2):
+                        store(part, b, slice(EARLY_HEADS, HEADS), (nc.scalar, nc.sync)[b])
+            first_bank += banks

@@ -89,7 +89,7 @@ def tile_attention_pa_k_kernel(tc, x, f1, f2, f3, Wqkv_words, Wqkv_scales, out_0
             if j == 0:
                 held_by = PASSES - SCALE_PIECE
                 nc.vector.tensor_copy(
-                    out=w_chunk[0:4, 0:4].bitcast(I32), in_=plane[0:4, held_by, 0:4].bitcast(I32)
+                    out=w_chunk[32:34, 0:4].bitcast(I32), in_=plane[32:34, held_by, 0:4].bitcast(I32)
                 )
             nc.sync.dma_start(
                 out=w_chunk[:, : groups * row].bitcast(I32).rearrange("p (g c) -> p g c", g=groups),

@@ -26,9 +26,12 @@ PART_BANKS = PART // BANK
 PSUM_BANKS = 8
 X_PIECE = 8
 SCALE_PIECE = 8
-ROUNDS = ((6, 1), (2, 4), (1, 4))
-AHEAD = 8
-LOAD_BYTES = 8192
+QK_BANKS = 2 * PART_BANKS
+V_BANKS = PART_BANKS
+SPLIT = 12
+V_GROUPS = 2
+LOAD_BYTES = 2 * BANK * QK_BANKS
+AHEAD = 11
 EARLY_HEADS = 2 * BANK // HEAD
 TABLE = BANK + (PART_BANKS - 1) * ROPE
 
@@ -75,12 +78,10 @@ def tile_attention_pa_k_kernel(tc, x, f1, f2, f3, Wqkv_words, Wqkv_scales, out_0
                     in_=scales_i32[gs, q:16:8, :].rearrange("g q c -> q g c"),
                 )
 
-        loads = []
-        first_bank = 0
-        for banks, groups in ROUNDS:
-            for g in range(0, PASSES, groups):
-                loads.append((first_bank, banks, g, groups))
-            first_bank += banks
+        loads = [(0, QK_BANKS, g, 1) for g in range(PASSES)]
+        loads += [(QK_BANKS, V_BANKS, g, V_GROUPS) for g in range(0, SPLIT, V_GROUPS)]
+        loads += [(QK_BANKS, V_BANKS - 1, g, V_GROUPS) for g in range(SPLIT, PASSES, V_GROUPS)]
+        loads += [(QK_BANKS + V_BANKS - 1, 1, g, V_GROUPS) for g in range(SPLIT, PASSES, V_GROUPS)]
 
         def load_weights(j):
             first, banks, g, groups = loads[j]
@@ -180,23 +181,15 @@ def tile_attention_pa_k_kernel(tc, x, f1, f2, f3, Wqkv_words, Wqkv_scales, out_0
             nc.vector.tensor_mul(out=partner_v[:, :, 1, :], in0=acc_v[:, :, 0, :], in1=sin_v[:, :, 1, :])
             nc.vector.tensor_add(out=results[part][:, cols], in0=own[:], in1=partner[:])
 
-        j = -1
-        first_bank = 0
-        for banks, groups in ROUNDS:
-            accs = []
-            for c in range(banks):
-                acc = psum.tile([P, BANK], F32, tag="bank")
-                accs.append(acc)
-            for g in range(PASSES):
-                if g % groups == 0:
-                    j += 1
-                    if j + AHEAD < len(loads):
-                        w_chunks.append(load_weights(j + AHEAD))
+        def multiply(accs, j):
+            first, banks, first_group, groups = loads[j]
+            for i in range(groups):
+                g = first_group + i
                 for c in range(banks):
-                    first_col = (first_bank + c) * BANK
-                    first_byte = 2 * BANK * (g % groups * banks + c)
+                    first_col = (first + c) * BANK
+                    first_byte = 2 * BANK * (i * banks + c)
                     nc.tensor.matmul_mx(
-                        out=accs[c][:],
+                        out=accs[first + c][:],
                         lhsT=x_codes[:, g, :].bitcast(FP8X4),
                         lhsT_scale=x_scales[:, g, :],
                         rhs=w_chunks[j][:, first_byte : first_byte + 2 * BANK].bitcast(FP4X4),
@@ -205,23 +198,38 @@ def tile_attention_pa_k_kernel(tc, x, f1, f2, f3, Wqkv_words, Wqkv_scales, out_0
                         stop=(g == PASSES - 1),
                     )
 
-            for c in range(banks):
-                bank = first_bank + c
-                part, place = divmod(bank, PART_BANKS)
-                cols = slice(place * BANK, (place + 1) * BANK)
-                if part < 2:
-                    rotate(bank, accs[c])
-                elif place == 0:
-                    nc.scalar.copy(out=results[part][:, cols], in_=accs[c][:])
-                else:
-                    nc.vector.tensor_copy(out=results[part][:, cols], in_=accs[c][:])
-                if part < 2 and place == PART_BANKS - 1:
-                    for b in range(2):
-                        store(part, b, slice(0, HEADS), (nc.scalar, nc.sync)[part])
-                elif bank == PARTS * PART_BANKS - 2:
-                    for b in range(2):
-                        store(part, b, slice(0, EARLY_HEADS), (nc.scalar, nc.sync)[b])
-                elif bank == PARTS * PART_BANKS - 1:
-                    for b in range(2):
-                        store(part, b, slice(EARLY_HEADS, HEADS), (nc.scalar, nc.sync)[b])
-            first_bank += banks
+        def finish(bank, acc):
+            part, place = divmod(bank, PART_BANKS)
+            cols = slice(place * BANK, (place + 1) * BANK)
+            if part < 2:
+                rotate(bank, acc)
+            elif place == 0:
+                nc.scalar.copy(out=results[part][:, cols], in_=acc[:])
+            else:
+                nc.vector.tensor_copy(out=results[part][:, cols], in_=acc[:])
+            if part < 2 and place == PART_BANKS - 1:
+                for b in range(2):
+                    store(part, b, slice(0, HEADS), (nc.scalar, nc.sync)[part])
+            elif part == 2 and place == 1:
+                for b in range(2):
+                    store(part, b, slice(0, EARLY_HEADS), (nc.scalar, nc.sync)[b])
+            elif part == 2 and place == 2:
+                for b in range(2):
+                    store(part, b, slice(EARLY_HEADS, HEADS), (nc.scalar, nc.sync)[b])
+
+        accs = {}
+        last_load = {}
+        for j, (first, banks, g, groups) in enumerate(loads):
+            for bank in range(first, first + banks):
+                last_load[bank] = j
+        for j, (first, banks, g, groups) in enumerate(loads):
+            if j + AHEAD < len(loads):
+                w_chunks.append(load_weights(j + AHEAD))
+            if g == 0:
+                for bank in range(first, first + banks):
+                    acc = psum.tile([P, BANK], F32, tag="bank")
+                    accs[bank] = acc
+            multiply(accs, j)
+            for bank in range(first, first + banks):
+                if last_load[bank] == j:
+                    finish(bank, accs[bank])

@@ -31,6 +31,7 @@ V_BANKS = PART_BANKS
 SPLIT = 12
 V_GROUPS = 2
 LOAD_BYTES = 2 * BANK * QK_BANKS
+EARLY = 2
 AHEAD = 11
 EARLY_HEADS = 2 * BANK // HEAD
 TABLE = BANK + (PART_BANKS - 1) * ROPE
@@ -67,17 +68,6 @@ def tile_attention_pa_k_kernel(tc, x, f1, f2, f3, Wqkv_words, Wqkv_scales, out_0
             nc.sync.dma_start(out=x_piece[:], in_=x_rows[:, cols])
             x_pieces.append(x_piece)
 
-        plane = keep.tile([P, PASSES, PARTS * PART], U8, align_bytes=64)
-        for piece in range(PASSES // SCALE_PIECE):
-            gs = slice(piece * SCALE_PIECE, (piece + 1) * SCALE_PIECE)
-            nc.vector.memset(plane[:, gs, :].bitcast(I32), 0)
-            for q in range(8):
-                row = 32 * (q // 4) + q % 4
-                nc.sync.dma_start(
-                    out=plane[row:P:64, gs, :].bitcast(I32),
-                    in_=scales_i32[gs, q:16:8, :].rearrange("g q c -> q g c"),
-                )
-
         loads = [(0, QK_BANKS, g, 1) for g in range(PASSES)]
         loads += [(QK_BANKS, V_BANKS, g, V_GROUPS) for g in range(0, SPLIT, V_GROUPS)]
         loads += [(QK_BANKS, V_BANKS - 1, g, V_GROUPS) for g in range(SPLIT, PASSES, V_GROUPS)]
@@ -87,7 +77,7 @@ def tile_attention_pa_k_kernel(tc, x, f1, f2, f3, Wqkv_words, Wqkv_scales, out_0
             first, banks, g, groups = loads[j]
             row = 2 * BANK * banks
             w_chunk = w_pool.tile([P, LOAD_BYTES], U8, align_bytes=64)
-            if j == 0:
+            if j == EARLY:
                 held_by = PASSES - SCALE_PIECE
                 nc.vector.tensor_copy(
                     out=w_chunk[32:34, 0:4].bitcast(I32), in_=plane[32:34, held_by, 0:4].bitcast(I32)
@@ -101,8 +91,19 @@ def tile_attention_pa_k_kernel(tc, x, f1, f2, f3, Wqkv_words, Wqkv_scales, out_0
             return w_chunk
 
         w_chunks = []
-        for j in range(AHEAD):
+        for j in range(EARLY):
             w_chunks.append(load_weights(j))
+
+        plane = keep.tile([P, PASSES, PARTS * PART], U8, align_bytes=64)
+        for piece in range(PASSES // SCALE_PIECE):
+            gs = slice(piece * SCALE_PIECE, (piece + 1) * SCALE_PIECE)
+            nc.vector.memset(plane[:, gs, :].bitcast(I32), 0)
+            for q in range(8):
+                row = 32 * (q // 4) + q % 4
+                nc.sync.dma_start(
+                    out=plane[row:P:64, gs, :].bitcast(I32),
+                    in_=scales_i32[gs, q:16:8, :].rearrange("g q c -> q g c"),
+                )
 
         halves = "p (a h j) -> p a h j"
         angles_v = angles[:].rearrange(halves, h=2, j=ROPE // 2)
@@ -153,6 +154,9 @@ def tile_attention_pa_k_kernel(tc, x, f1, f2, f3, Wqkv_words, Wqkv_scales, out_0
                 scales=x_scales[:, gs, :].rearrange("p g r -> p (g r)"),
                 in_=grouped[:].rearrange("p g r u -> p (g r u)").bitcast(BF16),
             )
+
+        for j in range(EARLY, AHEAD):
+            w_chunks.append(load_weights(j))
 
         results = []
         for part in range(PARTS):

from contextlib import ExitStack

import concourse.mybir as mybir
from concourse.masks import make_identity

F32 = mybir.dt.float32
BF16 = mybir.dt.bfloat16
I32 = mybir.dt.int32
U32 = mybir.dt.uint32
U8 = mybir.dt.uint8
FP8X4 = mybir.dt.float8_e4m3fn_x4
FP4X4 = mybir.dt.float4_e2m1fn_x4
SIN = mybir.ActivationFunctionType.Sin

P = 128
K = 8192
K_PASS = 512
PASSES = K // K_PASS
HEADS = 16
HEAD = 96
ROPE = 32
PARTS = 3
PART = HEADS * HEAD
BANK = 512
PART_BANKS = PART // BANK
PSUM_BANKS = 8
X_PIECE = 8
SCALE_PIECE = 8
QK_BANKS = 2 * PART_BANKS
V_BANKS = PART_BANKS
SPLIT = 12
V_GROUPS = 2
LOAD_BYTES = 2 * BANK * QK_BANKS
EARLY = 2
AHEAD = 11
EARLY_HEADS = 2 * BANK // HEAD
TABLE = BANK + (PART_BANKS - 1) * ROPE

FLOPS = 2 * P * K * PARTS * PART


def tile_attention_pa_k_kernel(tc, x, f1, f2, f3, Wqkv_words, Wqkv_scales, out_0, out_1, out_2):
    nc = tc.nc
    outs = (out_0, out_1, out_2)
    words_i32 = Wqkv_words.bitcast(I32)
    scales_i32 = Wqkv_scales.bitcast(I32)

    with ExitStack() as ctx:
        ctx.enter_context(tc.manual_schedule())
        keep = ctx.enter_context(tc.tile_pool(name="keep", bufs=1))
        x_pool = ctx.enter_context(tc.tile_pool(name="x_pool", bufs=PASSES // X_PIECE))
        stage = ctx.enter_context(tc.tile_pool(name="stage", bufs=2))
        w_pool = ctx.enter_context(tc.tile_pool(name="w_pool", bufs=AHEAD + 1))
        psum = ctx.enter_context(tc.psum_pool(name="psum", bufs=PSUM_BANKS))

        batch_rows = [slice(b, P, 2) for b in range(2)]

        angles = keep.tile([P, HEAD], BF16)
        for b in range(2):
            for a, f in enumerate((f1, f2, f3)):
                nc.scalar.dma_start(out=angles[batch_rows[b], a * ROPE : (a + 1) * ROPE], in_=f)

        x_rows = x.rearrange("b n k -> (b n) k")
        x_pieces = []
        for piece in range(PASSES // X_PIECE):
            x_piece = x_pool.tile([P, X_PIECE * K_PASS], BF16)
            cols = slice(piece * X_PIECE * K_PASS, (piece + 1) * X_PIECE * K_PASS)
            nc.sync.dma_start(out=x_piece[:], in_=x_rows[:, cols])
            x_pieces.append(x_piece)

        loads = [(0, QK_BANKS, g, 1) for g in range(PASSES)]
        loads += [(QK_BANKS, V_BANKS, g, V_GROUPS) for g in range(0, SPLIT, V_GROUPS)]
        loads += [(QK_BANKS, V_BANKS - 1, g, V_GROUPS) for g in range(SPLIT, PASSES, V_GROUPS)]
        loads += [(QK_BANKS + V_BANKS - 1, 1, g, V_GROUPS) for g in range(SPLIT, PASSES, V_GROUPS)]

        def load_weights(j):
            first, banks, g, groups = loads[j]
            row = 2 * BANK * banks
            w_chunk = w_pool.tile([P, LOAD_BYTES], U8, align_bytes=64)
            if j == EARLY:
                held_by = PASSES - SCALE_PIECE
                nc.vector.tensor_copy(
                    out=w_chunk[32:34, 0:4].bitcast(I32), in_=plane[32:34, held_by, 0:4].bitcast(I32)
                )
            nc.sync.dma_start(
                out=w_chunk[:, : groups * row].bitcast(I32).rearrange("p (g c) -> p g c", g=groups),
                in_=words_i32[
                    g : g + groups, :, first * BANK // 2 : (first + banks) * BANK // 2
                ].rearrange("g p c -> p g c"),
            )
            return w_chunk

        w_chunks = []
        for j in range(EARLY):
            w_chunks.append(load_weights(j))

        plane = keep.tile([P, PASSES, PARTS * PART], U8, align_bytes=64)
        for piece in range(PASSES // SCALE_PIECE):
            gs = slice(piece * SCALE_PIECE, (piece + 1) * SCALE_PIECE)
            nc.vector.memset(plane[:, gs, :].bitcast(I32), 0)
            for q in range(8):
                row = 32 * (q // 4) + q % 4
                nc.sync.dma_start(
                    out=plane[row:P:64, gs, :].bitcast(I32),
                    in_=scales_i32[gs, q:16:8, :].rearrange("g q c -> q g c"),
                )

        halves = "p (a h j) -> p a h j"
        angles_v = angles[:].rearrange(halves, h=2, j=ROPE // 2)
        sin_head = keep.tile([P, HEAD], F32)
        sin_head_v = sin_head[:].rearrange(halves, h=2, j=ROPE // 2)
        nc.scalar.activation(out=sin_head_v[:, :, 0, :], in_=angles_v[:, :, 0, :], func=SIN, scale=-1.0)
        nc.scalar.activation(out=sin_head_v[:, :, 1, :], in_=angles_v[:, :, 1, :], func=SIN, scale=1.0)
        cos_head = keep.tile([P, HEAD], F32)
        nc.scalar.activation(out=cos_head[:], in_=angles[:], func=SIN, scale=0.5)
        nc.vector.tensor_mul(out=cos_head[:], in0=cos_head[:], in1=cos_head[:])
        nc.vector.tensor_scalar(
            out=cos_head[:], in0=cos_head[:], scalar1=-2.0, scalar2=1.0,
            op0=mybir.AluOpType.mult, op1=mybir.AluOpType.add,
        )
        cos_tab = keep.tile([P, TABLE], F32)
        sin_tab = keep.tile([P, TABLE], F32)
        for tab, head in ((cos_tab, cos_head), (sin_tab, sin_head)):
            nc.vector.tensor_copy(
                out=tab[:].rearrange("p (w c) -> p w c", c=HEAD),
                in_=head[:].unsqueeze(1).to_broadcast([P, TABLE // HEAD, HEAD]),
            )

        ident = keep.tile([P, P], F32)
        make_identity(nc, ident[:])
        x_codes = keep.tile([P, PASSES, P], U32, align_bytes=64)
        x_scales = keep.tile([P, PASSES, P], U8, align_bytes=64)
        for piece, x_piece in enumerate(x_pieces):
            x_words = x_piece[:].bitcast(F32)
            grouped = stage.tile([P, X_PIECE, P, 2], F32, align_bytes=64)
            for pair in range(X_PIECE // 2):
                turned = psum.tile([P, 2, 2, P], F32, tag="bank")
                for i in range(2):
                    first_word = (2 * pair + i) * K_PASS // 2
                    for u in range(2):
                        nc.tensor.transpose(
                            turned[:, i, u, :],
                            x_words[:, first_word + u : first_word + K_PASS // 2 : 2],
                            ident[:],
                        )
                for i in range(2):
                    nc.scalar.copy(
                        out=grouped[:, 2 * pair + i, :, :].rearrange("p (n b) u -> p n b u", b=2),
                        in_=turned[:, i, :, :].rearrange("p u (b n) -> p n b u", b=2),
                    )
            gs = slice(piece * X_PIECE, (piece + 1) * X_PIECE)
            nc.vector.quantize_mx(
                out=x_codes[:, gs, :].rearrange("p g r -> p (g r)").bitcast(FP8X4),
                scales=x_scales[:, gs, :].rearrange("p g r -> p (g r)"),
                in_=grouped[:].rearrange("p g r u -> p (g r u)").bitcast(BF16),
            )

        for j in range(EARLY, AHEAD):
            w_chunks.append(load_weights(j))

        results = []
        for part in range(PARTS):
            result = keep.tile([P, PART], F32, name="result%d" % part)
            results.append(result)

        def store(part, b, heads, queue):
            queue.dma_start(
                out=outs[part][b, heads].rearrange("h n d -> n h d"),
                in_=results[part][batch_rows[b], heads.start * HEAD : heads.stop * HEAD].rearrange(
                    "n (h d) -> n h d", d=HEAD
                ),
            )

        def rotate(bank, acc):
            part, c = divmod(bank, PART_BANKS)
            cols = slice(c * BANK, (c + 1) * BANK)
            window = slice(c * ROPE, c * ROPE + BANK)
            acc_v = acc[:].rearrange(halves, h=2, j=ROPE // 2)
            sin_v = sin_tab[:, window].rearrange(halves, h=2, j=ROPE // 2)
            own = stage.tile([P, BANK], F32)
            partner = stage.tile([P, BANK], F32)
            partner_v = partner[:].rearrange(halves, h=2, j=ROPE // 2)
            nc.vector.tensor_mul(out=own[:], in0=acc[:], in1=cos_tab[:, window])
            nc.vector.tensor_mul(out=partner_v[:, :, 0, :], in0=acc_v[:, :, 1, :], in1=sin_v[:, :, 0, :])
            nc.vector.tensor_mul(out=partner_v[:, :, 1, :], in0=acc_v[:, :, 0, :], in1=sin_v[:, :, 1, :])
            nc.vector.tensor_add(out=results[part][:, cols], in0=own[:], in1=partner[:])

        def multiply(accs, j):
            first, banks, first_group, groups = loads[j]
            for i in range(groups):
                g = first_group + i
                for c in range(banks):
                    first_col = (first + c) * BANK
                    first_byte = 2 * BANK * (i * banks + c)
                    nc.tensor.matmul_mx(
                        out=accs[first + c][:],
                        lhsT=x_codes[:, g, :].bitcast(FP8X4),
                        lhsT_scale=x_scales[:, g, :],
                        rhs=w_chunks[j][:, first_byte : first_byte + 2 * BANK].bitcast(FP4X4),
                        rhs_scale=plane[:, g, first_col : first_col + BANK],
                        start=(g == 0),
                        stop=(g == PASSES - 1),
                    )

        def finish(bank, acc):
            part, place = divmod(bank, PART_BANKS)
            cols = slice(place * BANK, (place + 1) * BANK)
            if part < 2:
                rotate(bank, acc)
            elif place == 0:
                nc.scalar.copy(out=results[part][:, cols], in_=acc[:])
            else:
                nc.vector.tensor_copy(out=results[part][:, cols], in_=acc[:])
            if part < 2 and place == PART_BANKS - 1:
                for b in range(2):
                    store(part, b, slice(0, HEADS), (nc.scalar, nc.sync)[part])
            elif part == 2 and place == 1:
                for b in range(2):
                    store(part, b, slice(0, EARLY_HEADS), (nc.scalar, nc.sync)[b])
            elif part == 2 and place == 2:
                for b in range(2):
                    store(part, b, slice(EARLY_HEADS, HEADS), (nc.scalar, nc.sync)[b])

        accs = {}
        last_load = {}
        for j, (first, banks, g, groups) in enumerate(loads):
            for bank in range(first, first + banks):
                last_load[bank] = j
        for j, (first, banks, g, groups) in enumerate(loads):
            if j + AHEAD < len(loads):
                w_chunks.append(load_weights(j + AHEAD))
            if g == 0:
                for bank in range(first, first + banks):
                    acc = psum.tile([P, BANK], F32, tag="bank")
                    accs[bank] = acc
            multiply(accs, j)
            for bank in range(first, first + banks):
                if last_load[bank] == j:
                    finish(bank, accs[bank])
